import numpy as np
import ml_dtypes


def mxq(x, axis, fmt="e4m3"):
    dtype, down = {"e4m3": (ml_dtypes.float8_e4m3fn, 7), "e5m2": (ml_dtypes.float8_e5m2, 14)}[fmt]
    v = np.moveaxis(np.asarray(x, np.float32).astype(ml_dtypes.bfloat16).astype(np.float64), axis, -1)
    blocks = v.reshape(v.shape[:-1] + (-1, 32))
    amax = np.abs(blocks).max(-1, keepdims=True)
    byte = np.maximum(np.where(amax > 0, np.frexp(amax)[1] - 1 + 127, 0) - down, 1)
    scale = np.exp2(byte - 127.0)
    codes = (blocks / scale).astype(np.float32).astype(dtype).astype(np.float64)
    return np.moveaxis((codes * scale).reshape(v.shape), -1, axis)


WIDE = False


def mx_kscale(k):
    if not WIDE:
        return np.ones(k)
    levels = np.array([10, -10, 5, -5, 0])
    a = np.random.permutation(np.resize(levels, k // 512 * 4)).reshape(k // 512, 4)
    idx = np.arange(k)
    return np.exp2(a[idx // 512, idx % 128 // 32])


BF16 = ml_dtypes.bfloat16


def bf(x):
    return np.asarray(x, np.float32).astype(BF16)


def f64(x):
    return np.asarray(x).astype(np.float64)


B, S, HID, NH, NOPE, ROPE, VD, KV_RANK, SW, QB = 1, 8192, 512, 2, 64, 128, 128, 512, 384, 128


def rotate_half(x):
    h = x.shape[-1] // 2
    return np.concatenate([-x[..., h:], x[..., :h]], axis=-1)


def rope_tables():
    pos = np.arange(S, dtype=np.float64)
    inv = 1.0 / (10000.0 ** (np.arange(0, ROPE, 2, dtype=np.float64) / ROPE))
    ang = pos[:, None] * inv[None, :]
    ang = np.concatenate([ang, ang], axis=-1)
    return bf(np.broadcast_to(np.cos(ang)[None], (B, S, ROPE))), bf(np.broadcast_to(np.sin(ang)[None], (B, S, ROPE)))


def setup_inputs():
    s, t = mx_kscale(HID), mx_kscale(KV_RANK)
    col = np.concatenate([t, np.ones(ROPE)])
    cos, sin = rope_tables()
    return {"hidden_states": bf(np.random.standard_normal((B, S, HID)) * s), "cos": cos, "sin": sin,
            "Wkva": bf(np.random.standard_normal((HID, KV_RANK + ROPE)) / np.sqrt(HID) / s[:, None] * col),
            "bkva": bf(np.random.standard_normal(KV_RANK + ROPE) * 0.1 * col),
            "Wkvb": bf(np.random.standard_normal((KV_RANK, NH * (NOPE + VD))) / np.sqrt(KV_RANK) / t[:, None])}


def reference(hidden_states, cos, sin, Wkva, bkva, Wkvb):
    ckv = (mxq(f64(hidden_states), 2, "e4m3") @ mxq(f64(Wkva), 0, "e4m3")) + f64(bkva)
    kv_lat, k_rope = ckv[..., :KV_RANK], ckv[..., KV_RANK:]
    kv = (mxq(kv_lat, 2, "e4m3") @ mxq(f64(Wkvb), 0, "e4m3")).reshape(B, S, NH, NOPE + VD).transpose(0, 2, 1, 3)
    k_nope, v = kv[..., :NOPE], kv[..., NOPE:]
    k_rope = k_rope.reshape(B, 1, S, ROPE)
    c, si = f64(cos)[:, None], f64(sin)[:, None]
    k_rope = k_rope * c + rotate_half(k_rope) * si
    k_rope = np.broadcast_to(k_rope, (B, NH, S, ROPE))
    kk = np.concatenate([k_nope, k_rope], axis=-1)
    return kk, np.ascontiguousarray(v)

@@ -1,0 +1,336 @@
+from contextlib import ExitStack
+
+import concourse.mybir as mybir
+from concourse.masks import make_identity
+
+F32 = mybir.dt.float32
+BF16 = mybir.dt.bfloat16
+U32 = mybir.dt.uint32
+U8 = mybir.dt.uint8
+FP8X4 = mybir.dt.float8_e4m3fn_x4
+ADD = mybir.AluOpType.add
+SUB = mybir.AluOpType.subtract
+MUL = mybir.AluOpType.mult
+
+P = 128
+PACK = 4
+TOKENS = 8192
+HID = 512
+LATENT = 512
+ROPE = 128
+HALF = ROPE // 2
+NOPE = 64
+VDIM = 128
+HEADS = 2
+KK = NOPE + ROPE
+
+TILES = TOKENS // P
+ROUND = 4
+ROUNDS = TILES // ROUND
+CHUNK = 8
+CHUNKS = TILES // CHUNK
+ROUNDS_PER_CHUNK = CHUNK // ROUND
+TABLE_TILES = 32
+
+FLOPS = 2 * TOKENS * HID * (LATENT + ROPE) + 2 * TOKENS * LATENT * HEADS * (NOPE + VDIM)
+
+
+def tile_gptossmlaattention_pa_t_kernel(
+    tc, hidden_states, cos, sin, Wkva, bkva, Wkvb, out_0, out_1
+):
+    nc = tc.nc
+    with ExitStack() as ctx:
+        keep = ctx.enter_context(tc.tile_pool(name="keep", bufs=1))
+        work = ctx.enter_context(tc.tile_pool(name="work", bufs=2))
+        stage = ctx.enter_context(tc.tile_pool(name="stage", bufs=3))
+        psum = ctx.enter_context(tc.psum_pool(name="psum", bufs=4))
+        ctx.enter_context(tc.manual_schedule())
+
+        hs_view = hidden_states.flatten_outer_dims().rearrange("(p n) k -> p n k", n=TILES)
+        cos_view = cos.flatten_outer_dims().rearrange("(p n) d -> p n d", n=TILES)
+        sin_view = sin.flatten_outer_dims().rearrange("(p n) d -> p n d", n=TILES)
+        kk_view = out_0.rearrange("b h (p n) d -> p (b h) n d", n=TILES)
+        v_view = out_1.rearrange("b h (p n) d -> p (b h) n d", n=TILES)
+
+        wa_raw = keep.tile([P, PACK, LATENT + ROPE], BF16, name="wa_raw")
+        for u in range(2):
+            nc.sync.dma_start(
+                out=wa_raw[:, 2 * u : 2 * u + 2, :],
+                in_=Wkva[256 * u : 256 * u + 256, :].rearrange("(p e) c -> p e c", e=2),
+            )
+        hs_sb = [keep.tile([P, CHUNK, HID], BF16, name="hs%d" % c) for c in range(CHUNKS)]
+        cos_sb = [
+            keep.tile([P, TABLE_TILES, ROPE], BF16, name="cos%d" % g)
+            for g in range(TILES // TABLE_TILES)
+        ]
+        sin_sb = [
+            keep.tile([P, TABLE_TILES, ROPE], BF16, name="sin%d" % g)
+            for g in range(TILES // TABLE_TILES)
+        ]
+        wb_raw = keep.tile([P, PACK, HEADS * (NOPE + VDIM)], BF16, name="wb_raw")
+        bias_lat = keep.tile([P, PACK], BF16, name="bias_lat")
+        bias_rope = keep.tile([P, ROPE], BF16, name="bias_rope")
+        for c in range(CHUNKS):
+            nc.sync.dma_start(out=hs_sb[c][:], in_=hs_view[:, c * CHUNK : (c + 1) * CHUNK, :])
+            if c == 0:
+                nc.sync.dma_start(out=wb_raw[:], in_=Wkvb.rearrange("(p j) c -> p j c", j=PACK))
+                nc.sync.dma_start(
+                    out=bias_lat[:], in_=bkva[0:LATENT].rearrange("(m t) -> m t", t=PACK)
+                )
+                nc.sync.dma_start(
+                    out=bias_rope[:], in_=bkva[LATENT : LATENT + ROPE].partition_broadcast(P)
+                )
+            if c % (TABLE_TILES // CHUNK) == 1:
+                g = c * CHUNK // TABLE_TILES
+                rows = slice(g * TABLE_TILES, (g + 1) * TABLE_TILES)
+                nc.sync.dma_start(out=cos_sb[g][:], in_=cos_view[:, rows, :])
+                nc.sync.dma_start(out=sin_sb[g][:], in_=sin_view[:, rows, :])
+
+        ident = keep.tile([P, P], F32, name="ident")
+        make_identity(nc, ident[:])
+
+        wa_grp = keep.tile([P, LATENT + ROPE, PACK], BF16, name="wa_grp", align_bytes=64)
+        wa_codes = keep.tile([P, LATENT + ROPE], U32, name="wa_codes", align_bytes=64)
+        wa_scales = keep.tile([P, LATENT + ROPE], U8, name="wa_scales", align_bytes=64)
+        nc.vector.tensor_copy(
+            out=wa_grp[:, 0:LATENT, :].rearrange("p (t m) j -> p t m j", t=PACK),
+            in_=wa_raw[:, :, 0:LATENT].rearrange("p j (m t) -> p t m j", t=PACK),
+        )
+        nc.vector.tensor_copy(
+            out=wa_grp[:, LATENT:, :], in_=wa_raw[:, :, LATENT:].rearrange("p j c -> p c j")
+        )
+        for cols in (slice(0, LATENT), slice(LATENT, LATENT + ROPE)):
+            nc.vector.quantize_mx(
+                out=wa_codes[:, cols].bitcast(FP8X4),
+                scales=wa_scales[:, cols],
+                in_=wa_grp[:, cols, :].rearrange("p c j -> p (c j)"),
+            )
+        wb_grp = keep.tile([P, HEADS * (NOPE + VDIM), PACK], BF16, name="wb_grp", align_bytes=64)
+        wb_codes = keep.tile([P, HEADS * (NOPE + VDIM)], U32, name="wb_codes", align_bytes=64)
+        wb_scales = keep.tile([P, HEADS * (NOPE + VDIM)], U8, name="wb_scales", align_bytes=64)
+        V_COLS = slice(0, HEADS * VDIM)
+        NOPE_COLS = slice(HEADS * VDIM, HEADS * (VDIM + NOPE))
+        wb_by_head = wb_raw[:].rearrange("p j (h c) -> p h c j", h=HEADS)
+        nc.vector.tensor_copy(
+            out=wb_grp[:, V_COLS, :].rearrange("p (h c) j -> p h c j", h=HEADS),
+            in_=wb_by_head[:, :, NOPE:, :],
+        )
+        nc.vector.tensor_copy(
+            out=wb_grp[:, NOPE_COLS, :].rearrange("p (h c) j -> p h c j", h=HEADS),
+            in_=wb_by_head[:, :, 0:NOPE, :],
+        )
+        for cols in (V_COLS, NOPE_COLS):
+            nc.vector.quantize_mx(
+                out=wb_codes[:, cols].bitcast(FP8X4),
+                scales=wb_scales[:, cols],
+                in_=wb_grp[:, cols, :].rearrange("p c j -> p (c j)"),
+            )
+
+        hs_grouped = {}
+        hs_mx = {}
+        lat_bank = {}
+        lat_grouped = {}
+        lat_mx = {}
+        rope_bank = {}
+        rope_key = {}
+        kk_sb = {}
+        v_sb = {}
+
+        def transpose_hidden(r):
+            hs_grouped[r] = work.tile(
+                [P, ROUND * P * PACK], BF16, name="hs_grouped", tag="hs_grouped", bufs=3,
+                align_bytes=64,
+            )
+            words = hs_grouped[r][:].bitcast(F32).rearrange("p (i k u) -> p i k u", i=ROUND, u=2)
+            for a in range(ROUND // 2):
+                bank = psum.tile([P, 2, 2, P], F32, name="hs_bank", tag="scalar_ring")
+                for i in range(2):
+                    n = r * ROUND + 2 * a + i
+                    row_words = hs_sb[n // CHUNK][:, n % CHUNK, :].bitcast(F32)
+                    for u in range(2):
+                        nc.tensor.transpose(
+                            bank[:, i, u, :], row_words[:, u * P : (u + 1) * P], ident[:]
+                        )
+                nc.scalar.copy(
+                    out=words[:, 2 * a : 2 * a + 2, :, :],
+                    in_=bank[:].rearrange("p i u k -> p i k u"),
+                )
+
+        def quantise_hidden(r):
+            codes = work.tile(
+                [P, ROUND * P], U32, name="hs_codes", tag="hs_codes", bufs=3, align_bytes=64
+            )
+            scales = work.tile(
+                [P, ROUND * P], U8, name="hs_scales", tag="hs_scales", bufs=3, align_bytes=64
+            )
+            nc.vector.quantize_mx(
+                out=codes[:].bitcast(FP8X4), scales=scales[:], in_=hs_grouped[r][:]
+            )
+            hs_mx[r] = (codes, scales)
+
+        def latent_matmuls(r):
+            codes, scales = hs_mx[r]
+            for i in range(ROUND):
+                bank = psum.tile([P, PACK, P], F32, name="lat_bank", tag="vector_ring")
+                lat_bank[(r, i)] = bank
+                tokens = slice(i * P, (i + 1) * P)
+                for t in range(PACK):
+                    cols = slice(t * P, (t + 1) * P)
+                    nc.tensor.matmul_mx(
+                        out=bank[:, t, :],
+                        lhsT=wa_codes[:, cols].bitcast(FP8X4),
+                        lhsT_scale=wa_scales[:, cols],
+                        rhs=codes[:, tokens].bitcast(FP8X4),
+                        rhs_scale=scales[:, tokens],
+                        start=True,
+                        stop=True,
+                    )
+
+        def latent_out(r, i):
+            if i == 0:
+                lat_grouped[r] = work.tile(
+                    [P, ROUND, P, PACK], BF16, name="lat_grouped", tag="lat_grouped",
+                    align_bytes=64,
+                )
+            nc.vector.tensor_tensor(
+                out=lat_grouped[r][:, i, :, :],
+                in0=lat_bank[(r, i)][:].rearrange("p t k -> p k t"),
+                in1=bias_lat[:].unsqueeze(1).to_broadcast([P, P, PACK]),
+                op=ADD,
+            )
+
+        def quantise_latent(r):
+            codes = work.tile([P, ROUND * P], U32, name="lat_codes", tag="lat_codes", align_bytes=64)
+            scales = work.tile(
+                [P, ROUND * P], U8, name="lat_scales", tag="lat_scales", align_bytes=64
+            )
+            nc.vector.quantize_mx(
+                out=codes[:].bitcast(FP8X4),
+                scales=scales[:],
+                in_=lat_grouped[r][:].rearrange("p i k t -> p (i k t)"),
+            )
+            lat_mx[r] = (codes, scales)
+
+        def rope_matmuls(r):
+            codes, scales = hs_mx[r]
+            bank = psum.tile([P, ROUND, ROPE], F32, name="rope_bank", tag="vector_ring")
+            rope_bank[r] = bank
+            for i in range(ROUND):
+                tokens = slice(i * P, (i + 1) * P)
+                nc.tensor.matmul_mx(
+                    out=bank[:, i, :],
+                    lhsT=codes[:, tokens].bitcast(FP8X4),
+                    lhsT_scale=scales[:, tokens],
+                    rhs=wa_codes[:, LATENT:].bitcast(FP8X4),
+                    rhs_scale=wa_scales[:, LATENT:],
+                    start=True,
+                    stop=True,
+                )
+
+        def rope_out(r):
+            c, j = divmod(r * ROUND, CHUNK)
+            nc.vector.tensor_tensor(
+                out=rope_key[c][:, j : j + ROUND, :],
+                in0=rope_bank[r][:],
+                in1=bias_rope[:].unsqueeze(1).to_broadcast([P, ROUND, ROPE]),
+                op=ADD,
+            )
+
+        def second_product(r):
+            codes, scales = lat_mx[r]
+            c, j = divmod(r * ROUND, CHUNK)
+            for a in range(ROUND // 2):
+                bank = psum.tile([P, 2, HEADS, VDIM], F32, name="v_bank", tag="scalar_ring")
+                for i in range(2):
+                    tokens = slice((2 * a + i) * P, (2 * a + i + 1) * P)
+                    nc.tensor.matmul_mx(
+                        out=bank[:, i, :, :].rearrange("p h d -> p (h d)"),
+                        lhsT=codes[:, tokens].bitcast(FP8X4),
+                        lhsT_scale=scales[:, tokens],
+                        rhs=wb_codes[:, V_COLS].bitcast(FP8X4),
+                        rhs_scale=wb_scales[:, V_COLS],
+                        start=True,
+                        stop=True,
+                    )
+                nc.scalar.copy(
+                    out=v_sb[c][:, :, j + 2 * a : j + 2 * a + 2, :].rearrange("p h i d -> p i h d"),
+                    in_=bank[:],
+                )
+            bank = psum.tile([P, ROUND, HEADS, NOPE], F32, name="nope_bank", tag="scalar_ring")
+            for i in range(ROUND):
+                tokens = slice(i * P, (i + 1) * P)
+                nc.tensor.matmul_mx(
+                    out=bank[:, i, :, :].rearrange("p h d -> p (h d)"),
+                    lhsT=codes[:, tokens].bitcast(FP8X4),
+                    lhsT_scale=scales[:, tokens],
+                    rhs=wb_codes[:, NOPE_COLS].bitcast(FP8X4),
+                    rhs_scale=wb_scales[:, NOPE_COLS],
+                    start=True,
+                    stop=True,
+                )
+            nc.scalar.copy(
+                out=kk_sb[c][:, :, j : j + ROUND, 0:NOPE].rearrange("p h i d -> p i h d"),
+                in_=bank[:],
+            )
+
+        def rotate(c):
+            g, j = divmod(c * CHUNK, TABLE_TILES)
+            cos_c = cos_sb[g][:, j : j + CHUNK, :]
+            sin_c = sin_sb[g][:, j : j + CHUNK, :]
+            key = rope_key[c]
+            low, high = slice(0, HALF), slice(HALF, ROPE)
+            kk_low, kk_high = slice(NOPE, NOPE + HALF), slice(NOPE + HALF, KK)
+            head0, head1 = kk_sb[c][:, 0, :, :], kk_sb[c][:, 1, :, :]
+            nc.gpsimd.tensor_tensor(out=head0[:, :, NOPE:], in0=key[:], in1=cos_c, op=MUL)
+            nc.gpsimd.tensor_tensor(
+                out=head1[:, :, kk_low], in0=key[:, :, high], in1=sin_c[:, :, low], op=MUL
+            )
+            nc.gpsimd.tensor_tensor(
+                out=head1[:, :, kk_high], in0=key[:, :, low], in1=sin_c[:, :, high], op=MUL
+            )
+            nc.gpsimd.tensor_tensor(
+                out=head1[:, :, kk_low], in0=head0[:, :, kk_low], in1=head1[:, :, kk_low], op=SUB
+            )
+            nc.gpsimd.tensor_tensor(
+                out=head1[:, :, kk_high], in0=head0[:, :, kk_high], in1=head1[:, :, kk_high], op=ADD
+            )
+
+        def store_kk(c):
+            nc.scalar.copy(out=kk_sb[c][:, 0, :, NOPE:], in_=kk_sb[c][:, 1, :, NOPE:])
+            nc.sync.dma_start(out=kk_view[:, :, c * CHUNK : (c + 1) * CHUNK, :], in_=kk_sb[c][:])
+
+        def store_v(c):
+            nc.sync.dma_start(out=v_view[:, :, c * CHUNK : (c + 1) * CHUNK, :], in_=v_sb[c][:])
+
+        def live(r):
+            return 0 <= r < ROUNDS
+
+        for r in range(-3, ROUNDS + 3):
+            if live(r) and r % ROUNDS_PER_CHUNK == 0:
+                c = r // ROUNDS_PER_CHUNK
+                rope_key[c] = work.tile([P, CHUNK, ROPE], F32, name="rope_key", tag="rope_key")
+                kk_sb[c] = stage.tile([P, HEADS, CHUNK, KK], F32, name="kk_sb", tag="kk_sb")
+                v_sb[c] = stage.tile([P, HEADS, CHUNK, VDIM], F32, name="v_sb", tag="v_sb")
+            if live(r - 1):
+                second_product(r - 1)
+                if r % ROUNDS_PER_CHUNK == 0:
+                    store_v((r - 1) // ROUNDS_PER_CHUNK)
+            if live(r):
+                latent_out(r, 0)
+                rope_matmuls(r)
+            if live(r + 3):
+                transpose_hidden(r + 3)
+            if live(r):
+                for i in range(1, ROUND):
+                    latent_out(r, i)
+                rope_out(r)
+                if (r + 1) % ROUNDS_PER_CHUNK == 0:
+                    rotate(r // ROUNDS_PER_CHUNK)
+            if live(r + 1):
+                latent_matmuls(r + 1)
+            if live(r):
+                quantise_latent(r)
+            if live(r + 2):
+                quantise_hidden(r + 2)
+            if live(r - 2) and (r - 1) % ROUNDS_PER_CHUNK == 0:
+                store_kk((r - 2) // ROUNDS_PER_CHUNK)

@@ -27,9 +27,8 @@ KK = NOPE + ROPE
 TILES = TOKENS // P
 ROUND = 4
 ROUNDS = TILES // ROUND
-CHUNK = 8
+CHUNK = 2 * ROUND
 CHUNKS = TILES // CHUNK
-ROUNDS_PER_CHUNK = CHUNK // ROUND
 TABLE_TILES = 32
 
 FLOPS = 2 * TOKENS * HID * (LATENT + ROPE) + 2 * TOKENS * LATENT * HEADS * (NOPE + VDIM)
@@ -42,7 +41,6 @@ def tile_gptossmlaattention_pa_t_kernel(
     with ExitStack() as ctx:
         keep = ctx.enter_context(tc.tile_pool(name="keep", bufs=1))
         work = ctx.enter_context(tc.tile_pool(name="work", bufs=2))
-        stage = ctx.enter_context(tc.tile_pool(name="stage", bufs=3))
         psum = ctx.enter_context(tc.psum_pool(name="psum", bufs=4))
         ctx.enter_context(tc.manual_schedule())
 
@@ -52,12 +50,6 @@ def tile_gptossmlaattention_pa_t_kernel(
         kk_view = out_0.rearrange("b h (p n) d -> p (b h) n d", n=TILES)
         v_view = out_1.rearrange("b h (p n) d -> p (b h) n d", n=TILES)
 
-        wa_raw = keep.tile([P, PACK, LATENT + ROPE], BF16, name="wa_raw")
-        for u in range(2):
-            nc.sync.dma_start(
-                out=wa_raw[:, 2 * u : 2 * u + 2, :],
-                in_=Wkva[256 * u : 256 * u + 256, :].rearrange("(p e) c -> p e c", e=2),
-            )
         hs_sb = [keep.tile([P, CHUNK, HID], BF16, name="hs%d" % c) for c in range(CHUNKS)]
         cos_sb = [
             keep.tile([P, TABLE_TILES, ROPE], BF16, name="cos%d" % g)
@@ -67,64 +59,76 @@ def tile_gptossmlaattention_pa_t_kernel(
             keep.tile([P, TABLE_TILES, ROPE], BF16, name="sin%d" % g)
             for g in range(TILES // TABLE_TILES)
         ]
-        wb_raw = keep.tile([P, PACK, HEADS * (NOPE + VDIM)], BF16, name="wb_raw")
         bias_lat = keep.tile([P, PACK], BF16, name="bias_lat")
         bias_rope = keep.tile([P, ROPE], BF16, name="bias_rope")
-        for c in range(CHUNKS):
-            nc.sync.dma_start(out=hs_sb[c][:], in_=hs_view[:, c * CHUNK : (c + 1) * CHUNK, :])
-            if c == 0:
-                nc.sync.dma_start(out=wb_raw[:], in_=Wkvb.rearrange("(p j) c -> p j c", j=PACK))
-                nc.sync.dma_start(
-                    out=bias_lat[:], in_=bkva[0:LATENT].rearrange("(m t) -> m t", t=PACK)
-                )
-                nc.sync.dma_start(
-                    out=bias_rope[:], in_=bkva[LATENT : LATENT + ROPE].partition_broadcast(P)
-                )
-            if c % (TABLE_TILES // CHUNK) == 1:
-                g = c * CHUNK // TABLE_TILES
-                rows = slice(g * TABLE_TILES, (g + 1) * TABLE_TILES)
-                nc.sync.dma_start(out=cos_sb[g][:], in_=cos_view[:, rows, :])
-                nc.sync.dma_start(out=sin_sb[g][:], in_=sin_view[:, rows, :])
-
         ident = keep.tile([P, P], F32, name="ident")
-        make_identity(nc, ident[:])
-
-        wa_grp = keep.tile([P, LATENT + ROPE, PACK], BF16, name="wa_grp", align_bytes=64)
         wa_codes = keep.tile([P, LATENT + ROPE], U32, name="wa_codes", align_bytes=64)
         wa_scales = keep.tile([P, LATENT + ROPE], U8, name="wa_scales", align_bytes=64)
-        nc.vector.tensor_copy(
-            out=wa_grp[:, 0:LATENT, :].rearrange("p (t m) j -> p t m j", t=PACK),
-            in_=wa_raw[:, :, 0:LATENT].rearrange("p j (m t) -> p t m j", t=PACK),
-        )
-        nc.vector.tensor_copy(
-            out=wa_grp[:, LATENT:, :], in_=wa_raw[:, :, LATENT:].rearrange("p j c -> p c j")
-        )
-        for cols in (slice(0, LATENT), slice(LATENT, LATENT + ROPE)):
-            nc.vector.quantize_mx(
-                out=wa_codes[:, cols].bitcast(FP8X4),
-                scales=wa_scales[:, cols],
-                in_=wa_grp[:, cols, :].rearrange("p c j -> p (c j)"),
-            )
-        wb_grp = keep.tile([P, HEADS * (NOPE + VDIM), PACK], BF16, name="wb_grp", align_bytes=64)
         wb_codes = keep.tile([P, HEADS * (NOPE + VDIM)], U32, name="wb_codes", align_bytes=64)
         wb_scales = keep.tile([P, HEADS * (NOPE + VDIM)], U8, name="wb_scales", align_bytes=64)
+        LAT_COLS = slice(0, LATENT)
+        ROPE_COLS = slice(LATENT, LATENT + ROPE)
         V_COLS = slice(0, HEADS * VDIM)
         NOPE_COLS = slice(HEADS * VDIM, HEADS * (VDIM + NOPE))
-        wb_by_head = wb_raw[:].rearrange("p j (h c) -> p h c j", h=HEADS)
-        nc.vector.tensor_copy(
-            out=wb_grp[:, V_COLS, :].rearrange("p (h c) j -> p h c j", h=HEADS),
-            in_=wb_by_head[:, :, NOPE:, :],
-        )
-        nc.vector.tensor_copy(
-            out=wb_grp[:, NOPE_COLS, :].rearrange("p (h c) j -> p h c j", h=HEADS),
-            in_=wb_by_head[:, :, 0:NOPE, :],
-        )
-        for cols in (V_COLS, NOPE_COLS):
-            nc.vector.quantize_mx(
-                out=wb_codes[:, cols].bitcast(FP8X4),
-                scales=wb_scales[:, cols],
-                in_=wb_grp[:, cols, :].rearrange("p c j -> p (c j)"),
+
+        make_identity(nc, ident[:])
+
+        with tc.tile_pool(name="setup", bufs=1) as setup:
+            wa_raw = setup.tile([P, PACK, LATENT + ROPE], BF16, name="wa_raw")
+            for u in range(2):
+                nc.sync.dma_start(
+                    out=wa_raw[:, 2 * u : 2 * u + 2, :],
+                    in_=Wkva[256 * u : 256 * u + 256, :].rearrange("(p e) c -> p e c", e=2),
+                )
+            wb_raw = setup.tile([P, PACK, HEADS * (NOPE + VDIM)], BF16, name="wb_raw")
+            nc.sync.dma_start(out=wb_raw[:], in_=Wkvb.rearrange("(p j) c -> p j c", j=PACK))
+            nc.sync.dma_start(
+                out=bias_lat[:], in_=bkva[LAT_COLS].rearrange("(m t) -> m t", t=PACK)
             )
+            for c in range(CHUNKS):
+                nc.sync.dma_start(out=hs_sb[c][:], in_=hs_view[:, c * CHUNK : (c + 1) * CHUNK, :])
+                if c == 0:
+                    nc.sync.dma_start(out=bias_rope[:], in_=bkva[ROPE_COLS].partition_broadcast(P))
+                if c % (TABLE_TILES // CHUNK) == 1:
+                    g = c * CHUNK // TABLE_TILES
+                    rows = slice(g * TABLE_TILES, (g + 1) * TABLE_TILES)
+                    nc.sync.dma_start(out=cos_sb[g][:], in_=cos_view[:, rows, :])
+                    nc.sync.dma_start(out=sin_sb[g][:], in_=sin_view[:, rows, :])
+
+            wa_grp = setup.tile([P, LATENT + ROPE, PACK], BF16, name="wa_grp", align_bytes=64)
+            wb_grp = setup.tile(
+                [P, HEADS * (NOPE + VDIM), PACK], BF16, name="wb_grp", align_bytes=64
+            )
+            nc.vector.tensor_copy(
+                out=wa_grp[:, LAT_COLS, :].rearrange("p (t m) j -> p t m j", t=PACK),
+                in_=wa_raw[:, :, LAT_COLS].rearrange("p j (m t) -> p t m j", t=PACK),
+            )
+            nc.scalar.copy(
+                out=wa_grp[:, ROPE_COLS, :], in_=wa_raw[:, :, ROPE_COLS].rearrange("p j c -> p c j")
+            )
+            wb_by_head = wb_raw[:].rearrange("p j (h c) -> p h c j", h=HEADS)
+            nc.scalar.copy(
+                out=wb_grp[:, V_COLS, :].rearrange("p (h c) j -> p h c j", h=HEADS),
+                in_=wb_by_head[:, :, NOPE:, :],
+            )
+            nc.scalar.copy(
+                out=wb_grp[:, NOPE_COLS, :].rearrange("p (h c) j -> p h c j", h=HEADS),
+                in_=wb_by_head[:, :, 0:NOPE, :],
+            )
+            for cols in (LAT_COLS, ROPE_COLS):
+                nc.vector.quantize_mx(
+                    out=wa_codes[:, cols].bitcast(FP8X4),
+                    scales=wa_scales[:, cols],
+                    in_=wa_grp[:, cols, :].rearrange("p c j -> p (c j)"),
+                )
+            for cols in (V_COLS, NOPE_COLS):
+                nc.vector.quantize_mx(
+                    out=wb_codes[:, cols].bitcast(FP8X4),
+                    scales=wb_scales[:, cols],
+                    in_=wb_grp[:, cols, :].rearrange("p c j -> p (c j)"),
+                )
+
+        stage = ctx.enter_context(tc.tile_pool(name="stage", bufs=3))
 
         hs_grouped = {}
         hs_mx = {}
@@ -133,60 +137,72 @@ def tile_gptossmlaattention_pa_t_kernel(
         lat_mx = {}
         rope_bank = {}
         rope_key = {}
+        key_cos = {}
+        key_sin = {}
         kk_sb = {}
         v_sb = {}
 
+        def live(r):
+            return 0 <= r < ROUNDS
+
         def transpose_hidden(r):
+            if not live(r):
+                return
             hs_grouped[r] = work.tile(
-                [P, ROUND * P * PACK], BF16, name="hs_grouped", tag="hs_grouped", bufs=3,
+                [P, ROUND * P * PACK], BF16, name="hs_grouped", tag="hs_grouped", bufs=4,
                 align_bytes=64,
             )
             words = hs_grouped[r][:].bitcast(F32).rearrange("p (i k u) -> p i k u", i=ROUND, u=2)
-            for a in range(ROUND // 2):
+            for half in range(ROUND // 2):
                 bank = psum.tile([P, 2, 2, P], F32, name="hs_bank", tag="scalar_ring")
                 for i in range(2):
-                    n = r * ROUND + 2 * a + i
+                    n = r * ROUND + 2 * half + i
                     row_words = hs_sb[n // CHUNK][:, n % CHUNK, :].bitcast(F32)
                     for u in range(2):
                         nc.tensor.transpose(
                             bank[:, i, u, :], row_words[:, u * P : (u + 1) * P], ident[:]
                         )
                 nc.scalar.copy(
-                    out=words[:, 2 * a : 2 * a + 2, :, :],
+                    out=words[:, 2 * half : 2 * half + 2, :, :],
                     in_=bank[:].rearrange("p i u k -> p i k u"),
                 )
 
         def quantise_hidden(r):
+            if not live(r):
+                return
             codes = work.tile(
-                [P, ROUND * P], U32, name="hs_codes", tag="hs_codes", bufs=3, align_bytes=64
+                [P, ROUND * P], U32, name="hs_codes", tag="hs_codes", bufs=4, align_bytes=64
             )
             scales = work.tile(
-                [P, ROUND * P], U8, name="hs_scales", tag="hs_scales", bufs=3, align_bytes=64
+                [P, ROUND * P], U8, name="hs_scales", tag="hs_scales", bufs=4, align_bytes=64
             )
             nc.vector.quantize_mx(
                 out=codes[:].bitcast(FP8X4), scales=scales[:], in_=hs_grouped[r][:]
             )
             hs_mx[r] = (codes, scales)
 
-        def latent_matmuls(r):
+        def latent_matmuls(r, i):
+            if not live(r):
+                return
             codes, scales = hs_mx[r]
-            for i in range(ROUND):
-                bank = psum.tile([P, PACK, P], F32, name="lat_bank", tag="vector_ring")
-                lat_bank[(r, i)] = bank
-                tokens = slice(i * P, (i + 1) * P)
-                for t in range(PACK):
-                    cols = slice(t * P, (t + 1) * P)
-                    nc.tensor.matmul_mx(
-                        out=bank[:, t, :],
-                        lhsT=wa_codes[:, cols].bitcast(FP8X4),
-                        lhsT_scale=wa_scales[:, cols],
-                        rhs=codes[:, tokens].bitcast(FP8X4),
-                        rhs_scale=scales[:, tokens],
-                        start=True,
-                        stop=True,
-                    )
+            bank = psum.tile([P, PACK, P], F32, name="lat_bank", tag="vector_ring")
+            lat_bank[(r, i)] = bank
+            tokens = slice(i * P, (i + 1) * P)
+            for t in range(PACK):
+                cols = slice(t * P, (t + 1) * P)
+                nc.tensor.matmul_mx(
+                    out=bank[:, t, :],
+                    lhsT=wa_codes[:, cols].bitcast(FP8X4),
+                    lhsT_scale=wa_scales[:, cols],
+                    rhs=codes[:, tokens].bitcast(FP8X4),
+                    rhs_scale=scales[:, tokens],
+                    start=True,
+                    stop=True,
+                )
 
         def latent_out(r, i):
+            if not live(r):
+                return
             if i == 0:
                 lat_grouped[r] = work.tile(
                     [P, ROUND, P, PACK], BF16, name="lat_grouped", tag="lat_grouped",
@@ -200,6 +216,8 @@ def tile_gptossmlaattention_pa_t_kernel(
             )
 
         def quantise_latent(r):
+            if not live(r):
+                return
             codes = work.tile([P, ROUND * P], U32, name="lat_codes", tag="lat_codes", align_bytes=64)
             scales = work.tile(
                 [P, ROUND * P], U8, name="lat_scales", tag="lat_scales", align_bytes=64
@@ -212,6 +230,8 @@ def tile_gptossmlaattention_pa_t_kernel(
             lat_mx[r] = (codes, scales)
 
         def rope_matmuls(r):
+            if not live(r):
+                return
             codes, scales = hs_mx[r]
             bank = psum.tile([P, ROUND, ROPE], F32, name="rope_bank", tag="vector_ring")
             rope_bank[r] = bank
@@ -221,14 +241,18 @@ def tile_gptossmlaattention_pa_t_kernel(
                     out=bank[:, i, :],
                     lhsT=codes[:, tokens].bitcast(FP8X4),
                     lhsT_scale=scales[:, tokens],
-                    rhs=wa_codes[:, LATENT:].bitcast(FP8X4),
-                    rhs_scale=wa_scales[:, LATENT:],
+                    rhs=wa_codes[:, ROPE_COLS].bitcast(FP8X4),
+                    rhs_scale=wa_scales[:, ROPE_COLS],
                     start=True,
                     stop=True,
                 )
 
         def rope_out(r):
+            if not live(r):
+                return
             c, j = divmod(r * ROUND, CHUNK)
+            if j == 0:
+                rope_key[c] = work.tile([P, CHUNK, ROPE], F32, name="rope_key", tag="rope_key")
             nc.vector.tensor_tensor(
                 out=rope_key[c][:, j : j + ROUND, :],
                 in0=rope_bank[r][:],
@@ -236,13 +260,53 @@ def tile_gptossmlaattention_pa_t_kernel(
                 op=ADD,
             )
 
+        low, high = slice(0, HALF), slice(HALF, ROPE)
+
+        def rotate_products(c):
+            if not 0 <= c < CHUNKS:
+                return
+            g, j = divmod(c * CHUNK, TABLE_TILES)
+            cos_c = cos_sb[g][:, j : j + CHUNK, :]
+            sin_c = sin_sb[g][:, j : j + CHUNK, :]
+            key = rope_key[c]
+            key_cos[c] = work.tile([P, CHUNK, ROPE], F32, name="key_cos", tag="key_cos", bufs=1)
+            key_sin[c] = work.tile([P, CHUNK, ROPE], F32, name="key_sin", tag="key_sin", bufs=1)
+            nc.gpsimd.tensor_tensor(out=key_cos[c][:], in0=key[:], in1=cos_c, op=MUL)
+            nc.gpsimd.tensor_tensor(
+                out=key_sin[c][:, :, low], in0=key[:, :, high], in1=sin_c[:, :, low], op=MUL
+            )
+            nc.gpsimd.tensor_tensor(
+                out=key_sin[c][:, :, high], in0=key[:, :, low], in1=sin_c[:, :, high], op=MUL
+            )
+
+        def rotate_sum(c):
+            if not 0 <= c < CHUNKS:
+                return
+            kk_sb[c] = stage.tile([P, HEADS, CHUNK, KK], F32, name="kk_sb", tag="kk_sb")
+            nc.vector.tensor_tensor(
+                out=kk_sb[c][:, 1, :, NOPE : NOPE + HALF],
+                in0=key_cos[c][:, :, low],
+                in1=key_sin[c][:, :, low],
+                op=SUB,
+            )
+            nc.vector.tensor_tensor(
+                out=kk_sb[c][:, 1, :, NOPE + HALF :],
+                in0=key_cos[c][:, :, high],
+                in1=key_sin[c][:, :, high],
+                op=ADD,
+            )
+
         def second_product(r):
+            if not live(r):
+                return
             codes, scales = lat_mx[r]
             c, j = divmod(r * ROUND, CHUNK)
-            for a in range(ROUND // 2):
+            if j == 0:
+                v_sb[c] = stage.tile([P, HEADS, CHUNK, VDIM], F32, name="v_sb", tag="v_sb")
+            for half in range(ROUND // 2):
                 bank = psum.tile([P, 2, HEADS, VDIM], F32, name="v_bank", tag="scalar_ring")
                 for i in range(2):
-                    tokens = slice((2 * a + i) * P, (2 * a + i + 1) * P)
+                    tokens = slice((2 * half + i) * P, (2 * half + i + 1) * P)
                     nc.tensor.matmul_mx(
                         out=bank[:, i, :, :].rearrange("p h d -> p (h d)"),
                         lhsT=codes[:, tokens].bitcast(FP8X4),
@@ -252,8 +316,9 @@ def tile_gptossmlaattention_pa_t_kernel(
                         start=True,
                         stop=True,
                     )
+                first = j + 2 * half
                 nc.scalar.copy(
-                    out=v_sb[c][:, :, j + 2 * a : j + 2 * a + 2, :].rearrange("p h i d -> p i h d"),
+                    out=v_sb[c][:, :, first : first + 2, :].rearrange("p h i d -> p i h d"),
                     in_=bank[:],
                 )
             bank = psum.tile([P, ROUND, HEADS, NOPE], F32, name="nope_bank", tag="scalar_ring")
@@ -272,65 +337,37 @@ def tile_gptossmlaattention_pa_t_kernel(
                 out=kk_sb[c][:, :, j : j + ROUND, 0:NOPE].rearrange("p h i d -> p i h d"),
                 in_=bank[:],
             )
-
-        def rotate(c):
-            g, j = divmod(c * CHUNK, TABLE_TILES)
-            cos_c = cos_sb[g][:, j : j + CHUNK, :]
-            sin_c = sin_sb[g][:, j : j + CHUNK, :]
-            key = rope_key[c]
-            low, high = slice(0, HALF), slice(HALF, ROPE)
-            kk_low, kk_high = slice(NOPE, NOPE + HALF), slice(NOPE + HALF, KK)
-            head0, head1 = kk_sb[c][:, 0, :, :], kk_sb[c][:, 1, :, :]
-            nc.gpsimd.tensor_tensor(out=head0[:, :, NOPE:], in0=key[:], in1=cos_c, op=MUL)
-            nc.gpsimd.tensor_tensor(
-                out=head1[:, :, kk_low], in0=key[:, :, high], in1=sin_c[:, :, low], op=MUL
+            nc.scalar.copy(
+                out=kk_sb[c][:, 0, j : j + ROUND, NOPE:], in_=kk_sb[c][:, 1, j : j + ROUND, NOPE:]
             )
-            nc.gpsimd.tensor_tensor(
-                out=head1[:, :, kk_high], in0=key[:, :, low], in1=sin_c[:, :, high], op=MUL
-            )
-            nc.gpsimd.tensor_tensor(
-                out=head1[:, :, kk_low], in0=head0[:, :, kk_low], in1=head1[:, :, kk_low], op=SUB
-            )
-            nc.gpsimd.tensor_tensor(
-                out=head1[:, :, kk_high], in0=head0[:, :, kk_high], in1=head1[:, :, kk_high], op=ADD
-            )
+            tiles = slice(r * ROUND, (r + 1) * ROUND)
+            nc.sync.dma_start(out=v_view[:, :, tiles, :], in_=v_sb[c][:, :, j : j + ROUND, :])
+            nc.sync.dma_start(out=kk_view[:, :, tiles, :], in_=kk_sb[c][:, :, j : j + ROUND, :])
 
-        def store_kk(c):
-            nc.scalar.copy(out=kk_sb[c][:, 0, :, NOPE:], in_=kk_sb[c][:, 1, :, NOPE:])
-            nc.sync.dma_start(out=kk_view[:, :, c * CHUNK : (c + 1) * CHUNK, :], in_=kk_sb[c][:])
-
-        def store_v(c):
-            nc.sync.dma_start(out=v_view[:, :, c * CHUNK : (c + 1) * CHUNK, :], in_=v_sb[c][:])
-
-        def live(r):
-            return 0 <= r < ROUNDS
-
-        for r in range(-3, ROUNDS + 3):
-            if live(r) and r % ROUNDS_PER_CHUNK == 0:
-                c = r // ROUNDS_PER_CHUNK
-                rope_key[c] = work.tile([P, CHUNK, ROPE], F32, name="rope_key", tag="rope_key")
-                kk_sb[c] = stage.tile([P, HEADS, CHUNK, KK], F32, name="kk_sb", tag="kk_sb")
-                v_sb[c] = stage.tile([P, HEADS, CHUNK, VDIM], F32, name="v_sb", tag="v_sb")
-            if live(r - 1):
-                second_product(r - 1)
-                if r % ROUNDS_PER_CHUNK == 0:
-                    store_v((r - 1) // ROUNDS_PER_CHUNK)
-            if live(r):
-                latent_out(r, 0)
-                rope_matmuls(r)
-            if live(r + 3):
-                transpose_hidden(r + 3)
-            if live(r):
-                for i in range(1, ROUND):
-                    latent_out(r, i)
-                rope_out(r)
-                if (r + 1) % ROUNDS_PER_CHUNK == 0:
-                    rotate(r // ROUNDS_PER_CHUNK)
-            if live(r + 1):
-                latent_matmuls(r + 1)
-            if live(r):
-                quantise_latent(r)
-            if live(r + 2):
-                quantise_hidden(r + 2)
-            if live(r - 2) and (r - 1) % ROUNDS_PER_CHUNK == 0:
-                store_kk((r - 2) // ROUNDS_PER_CHUNK)
+        for c in range(-3, CHUNKS + 1):
+            a, b = 2 * c, 2 * c + 1
+            second_product(a - 2)
+            second_product(b - 2)
+            rotate_products(c)
+            for i in range(ROUND):
+                latent_out(a, i)
+                latent_matmuls(b, i)
+            latent_out(b, 0)
+            rope_matmuls(a + 2)
+            latent_out(b, 1)
+            rope_matmuls(b + 2)
+            transpose_hidden(a + 6)
+            transpose_hidden(b + 6)
+            latent_out(b, 2)
+            latent_matmuls(a + 2, 0)
+            latent_out(b, 3)
+            latent_matmuls(a + 2, 1)
+            rope_out(a + 2)
+            latent_matmuls(a + 2, 2)
+            rope_out(b + 2)
+            latent_matmuls(a + 2, 3)
+            quantise_latent(a)
+            quantise_latent(b)
+            quantise_hidden(a + 4)
+            quantise_hidden(b + 4)
+            rotate_sum(c)

@@ -29,7 +29,7 @@ ROUND = 4
 ROUNDS = TILES // ROUND
 CHUNK = 2 * ROUND
 CHUNKS = TILES // CHUNK
-TABLE_TILES = 32
+FILL_STEPS = 3
 
 FLOPS = 2 * TOKENS * HID * (LATENT + ROPE) + 2 * TOKENS * LATENT * HEADS * (NOPE + VDIM)
 
@@ -50,15 +50,9 @@ def tile_gptossmlaattention_pa_t_kernel(
         kk_view = out_0.rearrange("b h (p n) d -> p (b h) n d", n=TILES)
         v_view = out_1.rearrange("b h (p n) d -> p (b h) n d", n=TILES)
 
-        hs_sb = [keep.tile([P, CHUNK, HID], BF16, name="hs%d" % c) for c in range(CHUNKS)]
-        cos_sb = [
-            keep.tile([P, TABLE_TILES, ROPE], BF16, name="cos%d" % g)
-            for g in range(TILES // TABLE_TILES)
-        ]
-        sin_sb = [
-            keep.tile([P, TABLE_TILES, ROPE], BF16, name="sin%d" % g)
-            for g in range(TILES // TABLE_TILES)
-        ]
+        hs_sb = [keep.tile([P, ROUND, HID], BF16, name="hs%d" % r) for r in range(ROUNDS)]
+        cos_sb = [keep.tile([P, CHUNK, ROPE], BF16, name="cos%d" % c) for c in range(CHUNKS)]
+        sin_sb = [keep.tile([P, CHUNK, ROPE], BF16, name="sin%d" % c) for c in range(CHUNKS)]
         bias_lat = keep.tile([P, PACK], BF16, name="bias_lat")
         bias_rope = keep.tile([P, ROPE], BF16, name="bias_rope")
         ident = keep.tile([P, P], F32, name="ident")
@@ -82,18 +76,24 @@ def tile_gptossmlaattention_pa_t_kernel(
                 )
             wb_raw = setup.tile([P, PACK, HEADS * (NOPE + VDIM)], BF16, name="wb_raw")
             nc.sync.dma_start(out=wb_raw[:], in_=Wkvb.rearrange("(p j) c -> p j c", j=PACK))
+
+            def load_hidden(c):
+                for r in (2 * c, 2 * c + 1):
+                    tiles = slice(r * ROUND, (r + 1) * ROUND)
+                    nc.sync.dma_start(out=hs_sb[r][:], in_=hs_view[:, tiles, :])
+
+            load_hidden(0)
+            nc.sync.dma_start(out=bias_rope[:], in_=bkva[ROPE_COLS].partition_broadcast(P))
             nc.sync.dma_start(
                 out=bias_lat[:], in_=bkva[LAT_COLS].rearrange("(m t) -> m t", t=PACK)
             )
+            load_hidden(1)
             for c in range(CHUNKS):
-                nc.sync.dma_start(out=hs_sb[c][:], in_=hs_view[:, c * CHUNK : (c + 1) * CHUNK, :])
-                if c == 0:
-                    nc.sync.dma_start(out=bias_rope[:], in_=bkva[ROPE_COLS].partition_broadcast(P))
-                if c % (TABLE_TILES // CHUNK) == 1:
-                    g = c * CHUNK // TABLE_TILES
-                    rows = slice(g * TABLE_TILES, (g + 1) * TABLE_TILES)
-                    nc.sync.dma_start(out=cos_sb[g][:], in_=cos_view[:, rows, :])
-                    nc.sync.dma_start(out=sin_sb[g][:], in_=sin_view[:, rows, :])
+                if c + 2 < CHUNKS:
+                    load_hidden(c + 2)
+                tiles = slice(c * CHUNK, (c + 1) * CHUNK)
+                nc.sync.dma_start(out=cos_sb[c][:], in_=cos_view[:, tiles, :])
+                nc.sync.dma_start(out=sin_sb[c][:], in_=sin_view[:, tiles, :])
 
             wa_grp = setup.tile([P, LATENT + ROPE, PACK], BF16, name="wa_grp", align_bytes=64)
             wb_grp = setup.tile(
@@ -103,17 +103,8 @@ def tile_gptossmlaattention_pa_t_kernel(
                 out=wa_grp[:, LAT_COLS, :].rearrange("p (t m) j -> p t m j", t=PACK),
                 in_=wa_raw[:, :, LAT_COLS].rearrange("p j (m t) -> p t m j", t=PACK),
             )
-            nc.scalar.copy(
+            nc.vector.tensor_copy(
                 out=wa_grp[:, ROPE_COLS, :], in_=wa_raw[:, :, ROPE_COLS].rearrange("p j c -> p c j")
-            )
-            wb_by_head = wb_raw[:].rearrange("p j (h c) -> p h c j", h=HEADS)
-            nc.scalar.copy(
-                out=wb_grp[:, V_COLS, :].rearrange("p (h c) j -> p h c j", h=HEADS),
-                in_=wb_by_head[:, :, NOPE:, :],
-            )
-            nc.scalar.copy(
-                out=wb_grp[:, NOPE_COLS, :].rearrange("p (h c) j -> p h c j", h=HEADS),
-                in_=wb_by_head[:, :, 0:NOPE, :],
             )
             for cols in (LAT_COLS, ROPE_COLS):
                 nc.vector.quantize_mx(
@@ -121,6 +112,15 @@ def tile_gptossmlaattention_pa_t_kernel(
                     scales=wa_scales[:, cols],
                     in_=wa_grp[:, cols, :].rearrange("p c j -> p (c j)"),
                 )
+            wb_by_head = wb_raw[:].rearrange("p j (h c) -> p h c j", h=HEADS)
+            nc.vector.tensor_copy(
+                out=wb_grp[:, V_COLS, :].rearrange("p (h c) j -> p h c j", h=HEADS),
+                in_=wb_by_head[:, :, NOPE:, :],
+            )
+            nc.vector.tensor_copy(
+                out=wb_grp[:, NOPE_COLS, :].rearrange("p (h c) j -> p h c j", h=HEADS),
+                in_=wb_by_head[:, :, 0:NOPE, :],
+            )
             for cols in (V_COLS, NOPE_COLS):
                 nc.vector.quantize_mx(
                     out=wb_codes[:, cols].bitcast(FP8X4),
@@ -156,8 +156,7 @@ def tile_gptossmlaattention_pa_t_kernel(
             for half in range(ROUND // 2):
                 bank = psum.tile([P, 2, 2, P], F32, name="hs_bank", tag="scalar_ring")
                 for i in range(2):
-                    n = r * ROUND + 2 * half + i
-                    row_words = hs_sb[n // CHUNK][:, n % CHUNK, :].bitcast(F32)
+                    row_words = hs_sb[r][:, 2 * half + i, :].bitcast(F32)
                     for u in range(2):
                         nc.tensor.transpose(
                             bank[:, i, u, :], row_words[:, u * P : (u + 1) * P], ident[:]
@@ -265,18 +264,15 @@ def tile_gptossmlaattention_pa_t_kernel(
         def rotate_products(c):
             if not 0 <= c < CHUNKS:
                 return
-            g, j = divmod(c * CHUNK, TABLE_TILES)
-            cos_c = cos_sb[g][:, j : j + CHUNK, :]
-            sin_c = sin_sb[g][:, j : j + CHUNK, :]
             key = rope_key[c]
             key_cos[c] = work.tile([P, CHUNK, ROPE], F32, name="key_cos", tag="key_cos", bufs=1)
             key_sin[c] = work.tile([P, CHUNK, ROPE], F32, name="key_sin", tag="key_sin", bufs=1)
-            nc.gpsimd.tensor_tensor(out=key_cos[c][:], in0=key[:], in1=cos_c, op=MUL)
+            nc.gpsimd.tensor_tensor(out=key_cos[c][:], in0=key[:], in1=cos_sb[c][:], op=MUL)
             nc.gpsimd.tensor_tensor(
-                out=key_sin[c][:, :, low], in0=key[:, :, high], in1=sin_c[:, :, low], op=MUL
+                out=key_sin[c][:, :, low], in0=key[:, :, high], in1=sin_sb[c][:, :, low], op=MUL
             )
             nc.gpsimd.tensor_tensor(
-                out=key_sin[c][:, :, high], in0=key[:, :, low], in1=sin_c[:, :, high], op=MUL
+                out=key_sin[c][:, :, high], in0=key[:, :, low], in1=sin_sb[c][:, :, high], op=MUL
             )
 
         def rotate_sum(c):
@@ -344,7 +340,7 @@ def tile_gptossmlaattention_pa_t_kernel(
             nc.sync.dma_start(out=v_view[:, :, tiles, :], in_=v_sb[c][:, :, j : j + ROUND, :])
             nc.sync.dma_start(out=kk_view[:, :, tiles, :], in_=kk_sb[c][:, :, j : j + ROUND, :])
 
-        for c in range(-3, CHUNKS + 1):
+        for c in range(-FILL_STEPS, CHUNKS + 1):
             a, b = 2 * c, 2 * c + 1
             second_product(a - 2)
             second_product(b - 2)
@@ -356,8 +352,6 @@ def tile_gptossmlaattention_pa_t_kernel(
             rope_matmuls(a + 2)
             latent_out(b, 1)
             rope_matmuls(b + 2)
-            transpose_hidden(a + 6)
-            transpose_hidden(b + 6)
             latent_out(b, 2)
             latent_matmuls(a + 2, 0)
             latent_out(b, 3)
@@ -366,6 +360,8 @@ def tile_gptossmlaattention_pa_t_kernel(
             latent_matmuls(a + 2, 2)
             rope_out(b + 2)
             latent_matmuls(a + 2, 3)
+            transpose_hidden(a + 6)
+            transpose_hidden(b + 6)
             quantise_latent(a)
             quantise_latent(b)
             quantise_hidden(a + 4)

@@ -42,7 +42,6 @@ def tile_gptossmlaattention_pa_t_kernel(
         keep = ctx.enter_context(tc.tile_pool(name="keep", bufs=1))
         work = ctx.enter_context(tc.tile_pool(name="work", bufs=2))
         psum = ctx.enter_context(tc.psum_pool(name="psum", bufs=4))
-        ctx.enter_context(tc.manual_schedule())
 
         hs_view = hidden_states.flatten_outer_dims().rearrange("(p n) k -> p n k", n=TILES)
         cos_view = cos.flatten_outer_dims().rearrange("(p n) d -> p n d", n=TILES)

@@ -42,6 +42,7 @@ def tile_gptossmlaattention_pa_t_kernel(
         keep = ctx.enter_context(tc.tile_pool(name="keep", bufs=1))
         work = ctx.enter_context(tc.tile_pool(name="work", bufs=2))
         psum = ctx.enter_context(tc.psum_pool(name="psum", bufs=4))
+        ctx.enter_context(tc.manual_schedule())
 
         hs_view = hidden_states.flatten_outer_dims().rearrange("(p n) k -> p n k", n=TILES)
         cos_view = cos.flatten_outer_dims().rearrange("(p n) d -> p n d", n=TILES)
@@ -273,17 +274,17 @@ def tile_gptossmlaattention_pa_t_kernel(
             nc.gpsimd.tensor_tensor(
                 out=key_sin[c][:, :, high], in0=key[:, :, low], in1=sin_sb[c][:, :, high], op=MUL
             )
-
-        def rotate_sum(c):
-            if not 0 <= c < CHUNKS:
-                return
             kk_sb[c] = stage.tile([P, HEADS, CHUNK, KK], F32, name="kk_sb", tag="kk_sb")
-            nc.vector.tensor_tensor(
+            nc.gpsimd.tensor_tensor(
                 out=kk_sb[c][:, 1, :, NOPE : NOPE + HALF],
                 in0=key_cos[c][:, :, low],
                 in1=key_sin[c][:, :, low],
                 op=SUB,
             )
+
+        def rotate_high(c):
+            if not 0 <= c < CHUNKS:
+                return
             nc.vector.tensor_tensor(
                 out=kk_sb[c][:, 1, :, NOPE + HALF :],
                 in0=key_cos[c][:, :, high],
@@ -294,12 +295,16 @@ def tile_gptossmlaattention_pa_t_kernel(
         def second_product(r):
             if not live(r):
                 return
+            if r == ROUNDS - 1:
+                copy_out, ring = nc.vector.tensor_copy, "vector_ring"
+            else:
+                copy_out, ring = nc.scalar.copy, "scalar_ring"
             codes, scales = lat_mx[r]
             c, j = divmod(r * ROUND, CHUNK)
             if j == 0:
                 v_sb[c] = stage.tile([P, HEADS, CHUNK, VDIM], F32, name="v_sb", tag="v_sb")
             for half in range(ROUND // 2):
-                bank = psum.tile([P, 2, HEADS, VDIM], F32, name="v_bank", tag="scalar_ring")
+                bank = psum.tile([P, 2, HEADS, VDIM], F32, name="v_bank", tag=ring)
                 for i in range(2):
                     tokens = slice((2 * half + i) * P, (2 * half + i + 1) * P)
                     nc.tensor.matmul_mx(
@@ -312,11 +317,11 @@ def tile_gptossmlaattention_pa_t_kernel(
                         stop=True,
                     )
                 first = j + 2 * half
-                nc.scalar.copy(
+                copy_out(
                     out=v_sb[c][:, :, first : first + 2, :].rearrange("p h i d -> p i h d"),
                     in_=bank[:],
                 )
-            bank = psum.tile([P, ROUND, HEADS, NOPE], F32, name="nope_bank", tag="scalar_ring")
+            bank = psum.tile([P, ROUND, HEADS, NOPE], F32, name="nope_bank", tag=ring)
             for i in range(ROUND):
                 tokens = slice(i * P, (i + 1) * P)
                 nc.tensor.matmul_mx(
@@ -328,7 +333,7 @@ def tile_gptossmlaattention_pa_t_kernel(
                     start=True,
                     stop=True,
                 )
-            nc.scalar.copy(
+            copy_out(
                 out=kk_sb[c][:, :, j : j + ROUND, 0:NOPE].rearrange("p h i d -> p i h d"),
                 in_=bank[:],
             )
@@ -365,4 +370,4 @@ def tile_gptossmlaattention_pa_t_kernel(
             quantise_latent(b)
             quantise_hidden(a + 4)
             quantise_hidden(b + 4)
-            rotate_sum(c)
+            rotate_high(c)

from contextlib import ExitStack

import concourse.mybir as mybir
from concourse.masks import make_identity

F32 = mybir.dt.float32
BF16 = mybir.dt.bfloat16
U32 = mybir.dt.uint32
U8 = mybir.dt.uint8
FP8X4 = mybir.dt.float8_e4m3fn_x4
ADD = mybir.AluOpType.add
SUB = mybir.AluOpType.subtract
MUL = mybir.AluOpType.mult

P = 128
PACK = 4
TOKENS = 8192
HID = 512
LATENT = 512
ROPE = 128
HALF = ROPE // 2
NOPE = 64
VDIM = 128
HEADS = 2
KK = NOPE + ROPE

TILES = TOKENS // P
ROUND = 4
ROUNDS = TILES // ROUND
CHUNK = 2 * ROUND
CHUNKS = TILES // CHUNK
FILL_STEPS = 3

FLOPS = 2 * TOKENS * HID * (LATENT + ROPE) + 2 * TOKENS * LATENT * HEADS * (NOPE + VDIM)


def tile_gptossmlaattention_pa_t_kernel(
    tc, hidden_states, cos, sin, Wkva, bkva, Wkvb, out_0, out_1
):
    nc = tc.nc
    with ExitStack() as ctx:
        keep = ctx.enter_context(tc.tile_pool(name="keep", bufs=1))
        work = ctx.enter_context(tc.tile_pool(name="work", bufs=2))
        psum = ctx.enter_context(tc.psum_pool(name="psum", bufs=4))
        ctx.enter_context(tc.manual_schedule())

        hs_view = hidden_states.flatten_outer_dims().rearrange("(p n) k -> p n k", n=TILES)
        cos_view = cos.flatten_outer_dims().rearrange("(p n) d -> p n d", n=TILES)
        sin_view = sin.flatten_outer_dims().rearrange("(p n) d -> p n d", n=TILES)
        kk_view = out_0.rearrange("b h (p n) d -> p (b h) n d", n=TILES)
        v_view = out_1.rearrange("b h (p n) d -> p (b h) n d", n=TILES)

        hs_sb = [keep.tile([P, ROUND, HID], BF16, name="hs%d" % r) for r in range(ROUNDS)]
        cos_sb = [keep.tile([P, CHUNK, ROPE], BF16, name="cos%d" % c) for c in range(CHUNKS)]
        sin_sb = [keep.tile([P, CHUNK, ROPE], BF16, name="sin%d" % c) for c in range(CHUNKS)]
        bias_lat = keep.tile([P, PACK], BF16, name="bias_lat")
        bias_rope = keep.tile([P, ROPE], BF16, name="bias_rope")
        ident = keep.tile([P, P], F32, name="ident")
        wa_codes = keep.tile([P, LATENT + ROPE], U32, name="wa_codes", align_bytes=64)
        wa_scales = keep.tile([P, LATENT + ROPE], U8, name="wa_scales", align_bytes=64)
        wb_codes = keep.tile([P, HEADS * (NOPE + VDIM)], U32, name="wb_codes", align_bytes=64)
        wb_scales = keep.tile([P, HEADS * (NOPE + VDIM)], U8, name="wb_scales", align_bytes=64)
        LAT_COLS = slice(0, LATENT)
        ROPE_COLS = slice(LATENT, LATENT + ROPE)
        V_COLS = slice(0, HEADS * VDIM)
        NOPE_COLS = slice(HEADS * VDIM, HEADS * (VDIM + NOPE))

        make_identity(nc, ident[:])

        with tc.tile_pool(name="setup", bufs=1) as setup:
            wa_raw = setup.tile([P, PACK, LATENT + ROPE], BF16, name="wa_raw")
            for u in range(2):
                nc.sync.dma_start(
                    out=wa_raw[:, 2 * u : 2 * u + 2, :],
                    in_=Wkva[256 * u : 256 * u + 256, :].rearrange("(p e) c -> p e c", e=2),
                )
            wb_raw = setup.tile([P, PACK, HEADS * (NOPE + VDIM)], BF16, name="wb_raw")
            nc.sync.dma_start(out=wb_raw[:], in_=Wkvb.rearrange("(p j) c -> p j c", j=PACK))

            def load_hidden(c):
                for r in (2 * c, 2 * c + 1):
                    tiles = slice(r * ROUND, (r + 1) * ROUND)
                    nc.sync.dma_start(out=hs_sb[r][:], in_=hs_view[:, tiles, :])

            load_hidden(0)
            nc.sync.dma_start(out=bias_rope[:], in_=bkva[ROPE_COLS].partition_broadcast(P))
            nc.sync.dma_start(
                out=bias_lat[:], in_=bkva[LAT_COLS].rearrange("(m t) -> m t", t=PACK)
            )
            load_hidden(1)
            for c in range(CHUNKS):
                if c + 2 < CHUNKS:
                    load_hidden(c + 2)
                tiles = slice(c * CHUNK, (c + 1) * CHUNK)
                nc.sync.dma_start(out=cos_sb[c][:], in_=cos_view[:, tiles, :])
                nc.sync.dma_start(out=sin_sb[c][:], in_=sin_view[:, tiles, :])

            wa_grp = setup.tile([P, LATENT + ROPE, PACK], BF16, name="wa_grp", align_bytes=64)
            wb_grp = setup.tile(
                [P, HEADS * (NOPE + VDIM), PACK], BF16, name="wb_grp", align_bytes=64
            )
            nc.vector.tensor_copy(
                out=wa_grp[:, LAT_COLS, :].rearrange("p (t m) j -> p t m j", t=PACK),
                in_=wa_raw[:, :, LAT_COLS].rearrange("p j (m t) -> p t m j", t=PACK),
            )
            nc.vector.tensor_copy(
                out=wa_grp[:, ROPE_COLS, :], in_=wa_raw[:, :, ROPE_COLS].rearrange("p j c -> p c j")
            )
            for cols in (LAT_COLS, ROPE_COLS):
                nc.vector.quantize_mx(
                    out=wa_codes[:, cols].bitcast(FP8X4),
                    scales=wa_scales[:, cols],
                    in_=wa_grp[:, cols, :].rearrange("p c j -> p (c j)"),
                )
            wb_by_head = wb_raw[:].rearrange("p j (h c) -> p h c j", h=HEADS)
            nc.vector.tensor_copy(
                out=wb_grp[:, V_COLS, :].rearrange("p (h c) j -> p h c j", h=HEADS),
                in_=wb_by_head[:, :, NOPE:, :],
            )
            nc.vector.tensor_copy(
                out=wb_grp[:, NOPE_COLS, :].rearrange("p (h c) j -> p h c j", h=HEADS),
                in_=wb_by_head[:, :, 0:NOPE, :],
            )
            for cols in (V_COLS, NOPE_COLS):
                nc.vector.quantize_mx(
                    out=wb_codes[:, cols].bitcast(FP8X4),
                    scales=wb_scales[:, cols],
                    in_=wb_grp[:, cols, :].rearrange("p c j -> p (c j)"),
                )

        stage = ctx.enter_context(tc.tile_pool(name="stage", bufs=3))

        hs_grouped = {}
        hs_mx = {}
        lat_bank = {}
        lat_grouped = {}
        lat_mx = {}
        rope_bank = {}
        rope_key = {}
        key_cos = {}
        key_sin = {}
        kk_sb = {}
        v_sb = {}

        def live(r):
            return 0 <= r < ROUNDS

        def transpose_hidden(r):
            if not live(r):
                return
            hs_grouped[r] = work.tile(
                [P, ROUND * P * PACK], BF16, name="hs_grouped", tag="hs_grouped", bufs=4,
                align_bytes=64,
            )
            words = hs_grouped[r][:].bitcast(F32).rearrange("p (i k u) -> p i k u", i=ROUND, u=2)
            for half in range(ROUND // 2):
                bank = psum.tile([P, 2, 2, P], F32, name="hs_bank", tag="scalar_ring")
                for i in range(2):
                    row_words = hs_sb[r][:, 2 * half + i, :].bitcast(F32)
                    for u in range(2):
                        nc.tensor.transpose(
                            bank[:, i, u, :], row_words[:, u * P : (u + 1) * P], ident[:]
                        )
                nc.scalar.copy(
                    out=words[:, 2 * half : 2 * half + 2, :, :],
                    in_=bank[:].rearrange("p i u k -> p i k u"),
                )

        def quantise_hidden(r):
            if not live(r):
                return
            codes = work.tile(
                [P, ROUND * P], U32, name="hs_codes", tag="hs_codes", bufs=4, align_bytes=64
            )
            scales = work.tile(
                [P, ROUND * P], U8, name="hs_scales", tag="hs_scales", bufs=4, align_bytes=64
            )
            nc.vector.quantize_mx(
                out=codes[:].bitcast(FP8X4), scales=scales[:], in_=hs_grouped[r][:]
            )
            hs_mx[r] = (codes, scales)

        def latent_matmuls(r, i):
            if not live(r):
                return
            codes, scales = hs_mx[r]
            bank = psum.tile([P, PACK, P], F32, name="lat_bank", tag="vector_ring")
            lat_bank[(r, i)] = bank
            tokens = slice(i * P, (i + 1) * P)
            for t in range(PACK):
                cols = slice(t * P, (t + 1) * P)
                nc.tensor.matmul_mx(
                    out=bank[:, t, :],
                    lhsT=wa_codes[:, cols].bitcast(FP8X4),
                    lhsT_scale=wa_scales[:, cols],
                    rhs=codes[:, tokens].bitcast(FP8X4),
                    rhs_scale=scales[:, tokens],
                    start=True,
                    stop=True,
                )

        def latent_out(r, i):
            if not live(r):
                return
            if i == 0:
                lat_grouped[r] = work.tile(
                    [P, ROUND, P, PACK], BF16, name="lat_grouped", tag="lat_grouped",
                    align_bytes=64,
                )
            nc.vector.tensor_tensor(
                out=lat_grouped[r][:, i, :, :],
                in0=lat_bank[(r, i)][:].rearrange("p t k -> p k t"),
                in1=bias_lat[:].unsqueeze(1).to_broadcast([P, P, PACK]),
                op=ADD,
            )

        def quantise_latent(r):
            if not live(r):
                return
            codes = work.tile([P, ROUND * P], U32, name="lat_codes", tag="lat_codes", align_bytes=64)
            scales = work.tile(
                [P, ROUND * P], U8, name="lat_scales", tag="lat_scales", align_bytes=64
            )
            nc.vector.quantize_mx(
                out=codes[:].bitcast(FP8X4),
                scales=scales[:],
                in_=lat_grouped[r][:].rearrange("p i k t -> p (i k t)"),
            )
            lat_mx[r] = (codes, scales)

        def rope_matmuls(r):
            if not live(r):
                return
            codes, scales = hs_mx[r]
            bank = psum.tile([P, ROUND, ROPE], F32, name="rope_bank", tag="vector_ring")
            rope_bank[r] = bank
            for i in range(ROUND):
                tokens = slice(i * P, (i + 1) * P)
                nc.tensor.matmul_mx(
                    out=bank[:, i, :],
                    lhsT=codes[:, tokens].bitcast(FP8X4),
                    lhsT_scale=scales[:, tokens],
                    rhs=wa_codes[:, ROPE_COLS].bitcast(FP8X4),
                    rhs_scale=wa_scales[:, ROPE_COLS],
                    start=True,
                    stop=True,
                )

        def rope_out(r):
            if not live(r):
                return
            c, j = divmod(r * ROUND, CHUNK)
            if j == 0:
                rope_key[c] = work.tile([P, CHUNK, ROPE], F32, name="rope_key", tag="rope_key")
            nc.vector.tensor_tensor(
                out=rope_key[c][:, j : j + ROUND, :],
                in0=rope_bank[r][:],
                in1=bias_rope[:].unsqueeze(1).to_broadcast([P, ROUND, ROPE]),
                op=ADD,
            )

        low, high = slice(0, HALF), slice(HALF, ROPE)

        def rotate_products(c):
            if not 0 <= c < CHUNKS:
                return
            key = rope_key[c]
            key_cos[c] = work.tile([P, CHUNK, ROPE], F32, name="key_cos", tag="key_cos", bufs=1)
            key_sin[c] = work.tile([P, CHUNK, ROPE], F32, name="key_sin", tag="key_sin", bufs=1)
            nc.gpsimd.tensor_tensor(out=key_cos[c][:], in0=key[:], in1=cos_sb[c][:], op=MUL)
            nc.gpsimd.tensor_tensor(
                out=key_sin[c][:, :, low], in0=key[:, :, high], in1=sin_sb[c][:, :, low], op=MUL
            )
            nc.gpsimd.tensor_tensor(
                out=key_sin[c][:, :, high], in0=key[:, :, low], in1=sin_sb[c][:, :, high], op=MUL
            )
            kk_sb[c] = stage.tile([P, HEADS, CHUNK, KK], F32, name="kk_sb", tag="kk_sb")
            nc.gpsimd.tensor_tensor(
                out=kk_sb[c][:, 1, :, NOPE : NOPE + HALF],
                in0=key_cos[c][:, :, low],
                in1=key_sin[c][:, :, low],
                op=SUB,
            )

        def rotate_high(c):
            if not 0 <= c < CHUNKS:
                return
            nc.vector.tensor_tensor(
                out=kk_sb[c][:, 1, :, NOPE + HALF :],
                in0=key_cos[c][:, :, high],
                in1=key_sin[c][:, :, high],
                op=ADD,
            )

        def second_product(r):
            if not live(r):
                return
            if r == ROUNDS - 1:
                copy_out, ring = nc.vector.tensor_copy, "vector_ring"
            else:
                copy_out, ring = nc.scalar.copy, "scalar_ring"
            codes, scales = lat_mx[r]
            c, j = divmod(r * ROUND, CHUNK)
            if j == 0:
                v_sb[c] = stage.tile([P, HEADS, CHUNK, VDIM], F32, name="v_sb", tag="v_sb")
            for half in range(ROUND // 2):
                bank = psum.tile([P, 2, HEADS, VDIM], F32, name="v_bank", tag=ring)
                for i in range(2):
                    tokens = slice((2 * half + i) * P, (2 * half + i + 1) * P)
                    nc.tensor.matmul_mx(
                        out=bank[:, i, :, :].rearrange("p h d -> p (h d)"),
                        lhsT=codes[:, tokens].bitcast(FP8X4),
                        lhsT_scale=scales[:, tokens],
                        rhs=wb_codes[:, V_COLS].bitcast(FP8X4),
                        rhs_scale=wb_scales[:, V_COLS],
                        start=True,
                        stop=True,
                    )
                first = j + 2 * half
                copy_out(
                    out=v_sb[c][:, :, first : first + 2, :].rearrange("p h i d -> p i h d"),
                    in_=bank[:],
                )
            bank = psum.tile([P, ROUND, HEADS, NOPE], F32, name="nope_bank", tag=ring)
            for i in range(ROUND):
                tokens = slice(i * P, (i + 1) * P)
                nc.tensor.matmul_mx(
                    out=bank[:, i, :, :].rearrange("p h d -> p (h d)"),
                    lhsT=codes[:, tokens].bitcast(FP8X4),
                    lhsT_scale=scales[:, tokens],
                    rhs=wb_codes[:, NOPE_COLS].bitcast(FP8X4),
                    rhs_scale=wb_scales[:, NOPE_COLS],
                    start=True,
                    stop=True,
                )
            copy_out(
                out=kk_sb[c][:, :, j : j + ROUND, 0:NOPE].rearrange("p h i d -> p i h d"),
                in_=bank[:],
            )
            nc.scalar.copy(
                out=kk_sb[c][:, 0, j : j + ROUND, NOPE:], in_=kk_sb[c][:, 1, j : j + ROUND, NOPE:]
            )
            tiles = slice(r * ROUND, (r + 1) * ROUND)
            nc.sync.dma_start(out=v_view[:, :, tiles, :], in_=v_sb[c][:, :, j : j + ROUND, :])
            nc.sync.dma_start(out=kk_view[:, :, tiles, :], in_=kk_sb[c][:, :, j : j + ROUND, :])

        for c in range(-FILL_STEPS, CHUNKS + 1):
            a, b = 2 * c, 2 * c + 1
            second_product(a - 2)
            second_product(b - 2)
            rotate_products(c)
            for i in range(ROUND):
                latent_out(a, i)
                latent_matmuls(b, i)
            latent_out(b, 0)
            rope_matmuls(a + 2)
            latent_out(b, 1)
            rope_matmuls(b + 2)
            latent_out(b, 2)
            latent_matmuls(a + 2, 0)
            latent_out(b, 3)
            latent_matmuls(a + 2, 1)
            rope_out(a + 2)
            latent_matmuls(a + 2, 2)
            rope_out(b + 2)
            latent_matmuls(a + 2, 3)
            transpose_hidden(a + 6)
            transpose_hidden(b + 6)
            quantise_latent(a)
            quantise_latent(b)
            quantise_hidden(a + 4)
            quantise_hidden(b + 4)
            rotate_high(c)
